import numpy as np
import ml_dtypes

BF16 = ml_dtypes.bfloat16


def bf(x):
    return np.asarray(x, np.float32).astype(BF16)


def f32(x):
    return np.asarray(x, np.float32)


def f64(x):
    return np.asarray(x).astype(np.float64)


def striped(idx):
    return np.tile(idx.reshape(-1, 16).T, (8, 1))


C, S, NJ, KB, N, H, R = 128, 1024, 4, 128, 4096, 512, 8


def silu(v):
    return v / (1.0 + np.exp(-v))


def setup_inputs():
    atom_fea = f32(np.random.standard_normal((C, S)))
    w1 = bf(0.05 * np.random.standard_normal((C, C)))
    b1 = f32(0.1 * np.random.standard_normal((C, 1)))
    wenv = bf(0.1 * np.random.uniform(size=(KB, C)))
    rbf = bf(np.random.standard_normal((KB, N)))
    idx = np.concatenate([np.random.permutation(S)[:H] for _ in range(R)])
    return {"atom_fea": atom_fea, "w1": w1, "b1": b1, "wenv": wenv, "rbf": rbf, "offs": striped(idx)}


def reference(atom_fea, w1, b1, wenv, rbf, offs):
    idx = offs[:16].T.reshape(-1)
    t = f64(w1).T @ silu(f64(atom_fea)) + f64(b1)
    env = f64(wenv).T @ f64(rbf)
    prod = t[:, idx] * env
    return prod.reshape(C, NJ, S).sum(axis=1)

@@ -1,0 +1,67 @@
+import concourse.mybir as mybir
+
+F32 = mybir.dt.float32
+BF16 = mybir.dt.bfloat16
+U16 = mybir.dt.uint16
+MULT = mybir.AluOpType.mult
+ADD = mybir.AluOpType.add
+SILU = mybir.ActivationFunctionType.Silu
+
+P = 128
+ATOMS = 1024
+NEIGHBOURS = 4
+ENTRIES = NEIGHBOURS * ATOMS
+BANK = 512
+HALVES = ATOMS // BANK
+OFFSET_COLUMNS = ATOMS // 16
+
+FLOPS = 2 * P * P * ATOMS + 2 * P * P * ENTRIES
+
+
+def tile_spookylocalblock_kernel(tc, atom_fea, w1, b1, wenv, rbf, offs, out):
+    nc = tc.nc
+    with (
+        tc.tile_pool(name="held", bufs=1) as held,
+        tc.tile_pool(name="per_neighbour", bufs=NEIGHBOURS) as per_neighbour,
+        tc.psum_pool(name="t_banks", bufs=HALVES) as t_banks,
+        tc.psum_pool(name="env_banks", bufs=4) as env_banks,
+    ):
+        fea = held.tile([P, ATOMS], F32, name="fea")
+        nc.sync.dma_start(fea[:, 0:BANK], atom_fea[:, 0:BANK])
+        nc.scalar.dma_start(fea[:, BANK:ATOMS], atom_fea[:, BANK:ATOMS])
+        w1_sb = held.tile([P, P], BF16, name="w1_sb")
+        nc.gpsimd.dma_start(w1_sb[:], w1)
+        b1_sb = held.tile([P, 1], F32, name="b1_sb")
+        nc.gpsimd.dma_start(b1_sb[:], b1)
+        wenv_sb = held.tile([P, P], BF16, name="wenv_sb")
+        nc.gpsimd.dma_start(wenv_sb[:], wenv)
+        offsets = held.tile([P, ENTRIES // 16], U16, name="offsets")
+        nc.sync.dma_start(offsets[:], offs)
+
+        act = held.tile([P, ATOMS], BF16, name="act")
+        t = held.tile([P, ATOMS], F32, name="t")
+        for h in range(HALVES):
+            cols = slice(h * BANK, (h + 1) * BANK)
+            nc.scalar.activation(act[:, cols], fea[:, cols], SILU)
+            t_ps = t_banks.tile([P, BANK], F32, name="t_ps")
+            nc.tensor.matmul(t_ps[:], w1_sb[:], act[:, cols], start=True, stop=True)
+            nc.vector.tensor_scalar(t[:, cols], t_ps[:], b1_sb[:, 0:1], None, ADD)
+
+        total = held.tile([P, ATOMS], F32, name="total")
+        for n in range(NEIGHBOURS):
+            rbf_n = per_neighbour.tile([P, ATOMS], BF16, name="rbf_n")
+            nc.sync.dma_start(rbf_n[:], rbf[:, n * ATOMS : (n + 1) * ATOMS])
+            env_n = per_neighbour.tile([P, ATOMS], F32, name="env_n")
+            for h in range(HALVES):
+                cols = slice(h * BANK, (h + 1) * BANK)
+                env_ps = env_banks.tile([P, BANK], F32, name="env_ps")
+                nc.tensor.matmul(env_ps[:], wenv_sb[:], rbf_n[:, cols], start=True, stop=True)
+                nc.scalar.copy(env_n[:, cols], env_ps[:])
+            picked = t[:].indirect(offsets[:, n * OFFSET_COLUMNS : (n + 1) * OFFSET_COLUMNS])
+            if n == 0:
+                nc.vector.tensor_tensor(total[:], picked, env_n[:], MULT)
+            else:
+                prod_n = per_neighbour.tile([P, ATOMS], F32, name="prod_n")
+                nc.vector.tensor_tensor(prod_n[:], picked, env_n[:], MULT)
+                nc.vector.tensor_tensor(total[:], total[:], prod_n[:], ADD)
+        nc.sync.dma_start(out, total[:])

@@ -13,7 +13,8 @@ NEIGHBOURS = 4
 ENTRIES = NEIGHBOURS * ATOMS
 BANK = 512
 HALVES = ATOMS // BANK
-OFFSET_COLUMNS = ATOMS // 16
+PIECES = ENTRIES // BANK
+OFFSET_COLUMNS = BANK // 16
 
 FLOPS = 2 * P * P * ATOMS + 2 * P * P * ENTRIES
 
@@ -22,19 +23,19 @@ def tile_spookylocalblock_kernel(tc, atom_fea, w1, b1, wenv, rbf, offs, out):
     nc = tc.nc
     with (
         tc.tile_pool(name="held", bufs=1) as held,
-        tc.tile_pool(name="per_neighbour", bufs=NEIGHBOURS) as per_neighbour,
+        tc.tile_pool(name="per_piece", bufs=PIECES) as per_piece,
         tc.psum_pool(name="t_banks", bufs=HALVES) as t_banks,
         tc.psum_pool(name="env_banks", bufs=4) as env_banks,
     ):
+        w1_sb = held.tile([P, P], BF16, name="w1_sb")
+        nc.scalar.dma_start(w1_sb[:], w1)
         fea = held.tile([P, ATOMS], F32, name="fea")
         nc.sync.dma_start(fea[:, 0:BANK], atom_fea[:, 0:BANK])
         nc.scalar.dma_start(fea[:, BANK:ATOMS], atom_fea[:, BANK:ATOMS])
-        w1_sb = held.tile([P, P], BF16, name="w1_sb")
-        nc.gpsimd.dma_start(w1_sb[:], w1)
         b1_sb = held.tile([P, 1], F32, name="b1_sb")
-        nc.gpsimd.dma_start(b1_sb[:], b1)
+        nc.scalar.dma_start(b1_sb[:], b1)
         wenv_sb = held.tile([P, P], BF16, name="wenv_sb")
-        nc.gpsimd.dma_start(wenv_sb[:], wenv)
+        nc.scalar.dma_start(wenv_sb[:], wenv)
         offsets = held.tile([P, ENTRIES // 16], U16, name="offsets")
         nc.sync.dma_start(offsets[:], offs)
 
@@ -47,21 +48,22 @@ def tile_spookylocalblock_kernel(tc, atom_fea, w1, b1, wenv, rbf, offs, out):
             nc.tensor.matmul(t_ps[:], w1_sb[:], act[:, cols], start=True, stop=True)
             nc.vector.tensor_scalar(t[:, cols], t_ps[:], b1_sb[:, 0:1], None, ADD)
 
-        total = held.tile([P, ATOMS], F32, name="total")
-        for n in range(NEIGHBOURS):
-            rbf_n = per_neighbour.tile([P, ATOMS], BF16, name="rbf_n")
-            nc.sync.dma_start(rbf_n[:], rbf[:, n * ATOMS : (n + 1) * ATOMS])
-            env_n = per_neighbour.tile([P, ATOMS], F32, name="env_n")
-            for h in range(HALVES):
-                cols = slice(h * BANK, (h + 1) * BANK)
+        for h in range(HALVES):
+            for n in range(NEIGHBOURS):
+                k = n * HALVES + h
+                rbf_k = per_piece.tile([P, BANK], BF16, name="rbf_k")
+                nc.sync.dma_start(rbf_k[:], rbf[:, k * BANK : (k + 1) * BANK])
                 env_ps = env_banks.tile([P, BANK], F32, name="env_ps")
-                nc.tensor.matmul(env_ps[:], wenv_sb[:], rbf_n[:, cols], start=True, stop=True)
-                nc.scalar.copy(env_n[:, cols], env_ps[:])
-            picked = t[:].indirect(offsets[:, n * OFFSET_COLUMNS : (n + 1) * OFFSET_COLUMNS])
-            if n == 0:
-                nc.vector.tensor_tensor(total[:], picked, env_n[:], MULT)
-            else:
-                prod_n = per_neighbour.tile([P, ATOMS], F32, name="prod_n")
-                nc.vector.tensor_tensor(prod_n[:], picked, env_n[:], MULT)
-                nc.vector.tensor_tensor(total[:], total[:], prod_n[:], ADD)
-        nc.sync.dma_start(out, total[:])
+                nc.tensor.matmul(env_ps[:], wenv_sb[:], rbf_k[:], start=True, stop=True)
+                env_k = per_piece.tile([P, BANK], F32, name="env_k")
+                nc.scalar.copy(env_k[:], env_ps[:])
+                prod = per_piece.tile([P, BANK], F32, name="prod")
+                picked = t[:].indirect(offsets[:, k * OFFSET_COLUMNS : (k + 1) * OFFSET_COLUMNS])
+                nc.vector.tensor_tensor(prod[:], picked, env_k[:], MULT)
+                if n == 0:
+                    partial = prod
+                else:
+                    summed = per_piece.tile([P, BANK], F32, name="summed")
+                    nc.gpsimd.tensor_tensor(summed[:], partial[:], prod[:], ADD)
+                    partial = summed
+            nc.sync.dma_start(out[:, h * BANK : (h + 1) * BANK], partial[:])

@@ -1,4 +1,5 @@
 import concourse.mybir as mybir
+from concourse.masks import make_identity
 
 F32 = mybir.dt.float32
 BF16 = mybir.dt.bfloat16
@@ -23,47 +24,55 @@ def tile_spookylocalblock_kernel(tc, atom_fea, w1, b1, wenv, rbf, offs, out):
     nc = tc.nc
     with (
         tc.tile_pool(name="held", bufs=1) as held,
+        tc.tile_pool(name="per_half", bufs=HALVES) as per_half,
         tc.tile_pool(name="per_piece", bufs=PIECES) as per_piece,
         tc.psum_pool(name="t_banks", bufs=HALVES) as t_banks,
         tc.psum_pool(name="env_banks", bufs=4) as env_banks,
+        tc.psum_pool(name="out_banks", bufs=HALVES) as out_banks,
     ):
-        w1_sb = held.tile([P, P], BF16, name="w1_sb")
-        nc.scalar.dma_start(w1_sb[:], w1)
-        fea = held.tile([P, ATOMS], F32, name="fea")
-        nc.sync.dma_start(fea[:, 0:BANK], atom_fea[:, 0:BANK])
-        nc.scalar.dma_start(fea[:, BANK:ATOMS], atom_fea[:, BANK:ATOMS])
         b1_sb = held.tile([P, 1], F32, name="b1_sb")
-        nc.scalar.dma_start(b1_sb[:], b1)
+        nc.sync.dma_start(b1_sb[:], b1)
+        w1_sb = held.tile([P, P], BF16, name="w1_sb")
+        nc.sync.dma_start(w1_sb[:], w1)
+
+        identity = held.tile([P, P], F32, name="identity")
+        make_identity(nc, identity[:])
+
+        t = held.tile([P, ATOMS], F32, name="t")
+        for h, queue in enumerate((nc.sync, nc.scalar)):
+            cols = slice(h * BANK, (h + 1) * BANK)
+            fea = per_half.tile([P, BANK], F32, name="fea")
+            queue.dma_start(fea[:], atom_fea[:, cols])
+            act = per_half.tile([P, BANK], BF16, name="act")
+            nc.scalar.activation(act[:], fea[:], SILU)
+            t_ps = t_banks.tile([P, BANK], F32, name="t_ps")
+            nc.tensor.matmul(t_ps[:], w1_sb[:], act[:], start=True, stop=True)
+            nc.vector.tensor_scalar(t[:, cols], t_ps[:], b1_sb[:, 0:1], None, ADD)
+
         wenv_sb = held.tile([P, P], BF16, name="wenv_sb")
         nc.scalar.dma_start(wenv_sb[:], wenv)
         offsets = held.tile([P, ENTRIES // 16], U16, name="offsets")
         nc.sync.dma_start(offsets[:], offs)
 
-        act = held.tile([P, ATOMS], BF16, name="act")
-        t = held.tile([P, ATOMS], F32, name="t")
-        for h in range(HALVES):
-            cols = slice(h * BANK, (h + 1) * BANK)
-            nc.scalar.activation(act[:, cols], fea[:, cols], SILU)
-            t_ps = t_banks.tile([P, BANK], F32, name="t_ps")
-            nc.tensor.matmul(t_ps[:], w1_sb[:], act[:, cols], start=True, stop=True)
-            nc.vector.tensor_scalar(t[:, cols], t_ps[:], b1_sb[:, 0:1], None, ADD)
+        order = [n * HALVES + h for h in range(HALVES) for n in range(NEIGHBOURS)]
+
+        env = {}
+        for k in order:
+            rbf_k = per_piece.tile([P, BANK], BF16, name="rbf_k")
+            nc.sync.dma_start(rbf_k[:], rbf[:, k * BANK : (k + 1) * BANK])
+            env_ps = env_banks.tile([P, BANK], F32, name="env_ps")
+            nc.tensor.matmul(env_ps[:], wenv_sb[:], rbf_k[:], start=True, stop=True)
+            env[k] = per_piece.tile([P, BANK], F32, name="env_k")
+            nc.scalar.copy(env[k][:], env_ps[:])
 
         for h in range(HALVES):
+            out_ps = out_banks.tile([P, BANK], F32, name="out_ps")
             for n in range(NEIGHBOURS):
                 k = n * HALVES + h
-                rbf_k = per_piece.tile([P, BANK], BF16, name="rbf_k")
-                nc.sync.dma_start(rbf_k[:], rbf[:, k * BANK : (k + 1) * BANK])
-                env_ps = env_banks.tile([P, BANK], F32, name="env_ps")
-                nc.tensor.matmul(env_ps[:], wenv_sb[:], rbf_k[:], start=True, stop=True)
-                env_k = per_piece.tile([P, BANK], F32, name="env_k")
-                nc.scalar.copy(env_k[:], env_ps[:])
                 prod = per_piece.tile([P, BANK], F32, name="prod")
                 picked = t[:].indirect(offsets[:, k * OFFSET_COLUMNS : (k + 1) * OFFSET_COLUMNS])
-                nc.vector.tensor_tensor(prod[:], picked, env_k[:], MULT)
-                if n == 0:
-                    partial = prod
-                else:
-                    summed = per_piece.tile([P, BANK], F32, name="summed")
-                    nc.gpsimd.tensor_tensor(summed[:], partial[:], prod[:], ADD)
-                    partial = summed
-            nc.sync.dma_start(out[:, h * BANK : (h + 1) * BANK], partial[:])
+                nc.vector.tensor_tensor(prod[:], picked, env[k][:], MULT)
+                nc.tensor.matmul(out_ps[:], identity[:], prod[:], start=(n == 0), stop=(n == NEIGHBOURS - 1))
+            out_sb = per_half.tile([P, BANK], F32, name="out_sb")
+            nc.scalar.copy(out_sb[:], out_ps[:])
+            nc.sync.dma_start(out[:, h * BANK : (h + 1) * BANK], out_sb[:])

@@ -26,53 +26,57 @@ def tile_spookylocalblock_kernel(tc, atom_fea, w1, b1, wenv, rbf, offs, out):
         tc.tile_pool(name="held", bufs=1) as held,
         tc.tile_pool(name="per_half", bufs=HALVES) as per_half,
         tc.tile_pool(name="per_piece", bufs=PIECES) as per_piece,
-        tc.psum_pool(name="t_banks", bufs=HALVES) as t_banks,
-        tc.psum_pool(name="env_banks", bufs=4) as env_banks,
+        tc.psum_pool(name="banks", bufs=6) as banks,
         tc.psum_pool(name="out_banks", bufs=HALVES) as out_banks,
     ):
-        b1_sb = held.tile([P, 1], F32, name="b1_sb")
-        nc.sync.dma_start(b1_sb[:], b1)
+        fea = []
+        for h in range(HALVES):
+            fea.append(per_half.tile([P, BANK], F32, name="fea"))
+            nc.sync.dma_start(fea[h][:], atom_fea[:, h * BANK : (h + 1) * BANK])
         w1_sb = held.tile([P, P], BF16, name="w1_sb")
         nc.sync.dma_start(w1_sb[:], w1)
+        b1_sb = held.tile([P, 1], F32, name="b1_sb")
+        nc.sync.dma_start(b1_sb[:], b1)
+        wenv_sb = held.tile([P, P], BF16, name="wenv_sb")
+        nc.sync.dma_start(wenv_sb[:], wenv)
+        offsets = held.tile([P, ENTRIES // 16], U16, name="offsets")
+        nc.sync.dma_start(offsets[:], offs)
+        rbf_by_half = rbf.rearrange("q (n h b) -> q h n b", h=HALVES, b=BANK)
+        rbf_half = []
+        for h in range(HALVES):
+            rbf_half.append(per_half.tile([P, NEIGHBOURS, BANK], BF16, name="rbf_half"))
+            nc.sync.dma_start(rbf_half[h][:], rbf_by_half[:, h])
 
         identity = held.tile([P, P], F32, name="identity")
         make_identity(nc, identity[:])
 
         t = held.tile([P, ATOMS], F32, name="t")
-        for h, queue in enumerate((nc.sync, nc.scalar)):
-            cols = slice(h * BANK, (h + 1) * BANK)
-            fea = per_half.tile([P, BANK], F32, name="fea")
-            queue.dma_start(fea[:], atom_fea[:, cols])
+        for h in range(HALVES):
             act = per_half.tile([P, BANK], BF16, name="act")
-            nc.scalar.activation(act[:], fea[:], SILU)
-            t_ps = t_banks.tile([P, BANK], F32, name="t_ps")
+            nc.scalar.activation(act[:], fea[h][:], SILU)
+            t_ps = banks.tile([P, BANK], F32, name="t_ps", tag="bank")
             nc.tensor.matmul(t_ps[:], w1_sb[:], act[:], start=True, stop=True)
-            nc.vector.tensor_scalar(t[:, cols], t_ps[:], b1_sb[:, 0:1], None, ADD)
-
-        wenv_sb = held.tile([P, P], BF16, name="wenv_sb")
-        nc.scalar.dma_start(wenv_sb[:], wenv)
-        offsets = held.tile([P, ENTRIES // 16], U16, name="offsets")
-        nc.sync.dma_start(offsets[:], offs)
-
-        order = [n * HALVES + h for h in range(HALVES) for n in range(NEIGHBOURS)]
+            nc.vector.tensor_scalar(t[:, h * BANK : (h + 1) * BANK], t_ps[:], b1_sb[:, 0:1], None, ADD)
 
         env = {}
-        for k in order:
-            rbf_k = per_piece.tile([P, BANK], BF16, name="rbf_k")
-            nc.sync.dma_start(rbf_k[:], rbf[:, k * BANK : (k + 1) * BANK])
-            env_ps = env_banks.tile([P, BANK], F32, name="env_ps")
-            nc.tensor.matmul(env_ps[:], wenv_sb[:], rbf_k[:], start=True, stop=True)
-            env[k] = per_piece.tile([P, BANK], F32, name="env_k")
-            nc.scalar.copy(env[k][:], env_ps[:])
+        for h in range(HALVES):
+            for n in range(NEIGHBOURS):
+                env_ps = banks.tile([P, BANK], F32, name="env_ps", tag="bank")
+                nc.tensor.matmul(env_ps[:], wenv_sb[:], rbf_half[h][:, n, :], start=True, stop=True)
+                env[h, n] = per_piece.tile([P, BANK], F32, name="env_piece")
+                nc.scalar.copy(env[h, n][:], env_ps[:])
 
         for h in range(HALVES):
+            on_tensor = NEIGHBOURS - 1
             out_ps = out_banks.tile([P, BANK], F32, name="out_ps")
+            out_sb = per_half.tile([P, BANK], F32, name="out_sb")
             for n in range(NEIGHBOURS):
                 k = n * HALVES + h
                 prod = per_piece.tile([P, BANK], F32, name="prod")
                 picked = t[:].indirect(offsets[:, k * OFFSET_COLUMNS : (k + 1) * OFFSET_COLUMNS])
-                nc.vector.tensor_tensor(prod[:], picked, env[k][:], MULT)
-                nc.tensor.matmul(out_ps[:], identity[:], prod[:], start=(n == 0), stop=(n == NEIGHBOURS - 1))
-            out_sb = per_half.tile([P, BANK], F32, name="out_sb")
-            nc.scalar.copy(out_sb[:], out_ps[:])
+                nc.vector.tensor_tensor(prod[:], picked, env[h, n][:], MULT)
+                if n < on_tensor:
+                    nc.tensor.matmul(out_ps[:], identity[:], prod[:], start=(n == 0), stop=(n == on_tensor - 1))
+                else:
+                    nc.vector.tensor_tensor(out_sb[:], out_ps[:], prod[:], ADD)
             nc.sync.dma_start(out[:, h * BANK : (h + 1) * BANK], out_sb[:])

@@ -15,6 +15,7 @@ ENTRIES = NEIGHBOURS * ATOMS
 BANK = 512
 HALVES = ATOMS // BANK
 PIECES = ENTRIES // BANK
+PSUM_BANKS = 8
 OFFSET_COLUMNS = BANK // 16
 
 FLOPS = 2 * P * P * ATOMS + 2 * P * P * ENTRIES
@@ -25,9 +26,10 @@ def tile_spookylocalblock_kernel(tc, atom_fea, w1, b1, wenv, rbf, offs, out):
     with (
         tc.tile_pool(name="held", bufs=1) as held,
         tc.tile_pool(name="per_half", bufs=HALVES) as per_half,
+        tc.tile_pool(name="per_neighbour", bufs=NEIGHBOURS) as per_neighbour,
         tc.tile_pool(name="per_piece", bufs=PIECES) as per_piece,
-        tc.psum_pool(name="banks", bufs=6) as banks,
         tc.psum_pool(name="out_banks", bufs=HALVES) as out_banks,
+        tc.psum_pool(name="banks", bufs=PSUM_BANKS - HALVES) as banks,
     ):
         fea = []
         for h in range(HALVES):
@@ -41,11 +43,10 @@ def tile_spookylocalblock_kernel(tc, atom_fea, w1, b1, wenv, rbf, offs, out):
         nc.sync.dma_start(wenv_sb[:], wenv)
         offsets = held.tile([P, ENTRIES // 16], U16, name="offsets")
         nc.sync.dma_start(offsets[:], offs)
-        rbf_by_half = rbf.rearrange("q (n h b) -> q h n b", h=HALVES, b=BANK)
-        rbf_half = []
-        for h in range(HALVES):
-            rbf_half.append(per_half.tile([P, NEIGHBOURS, BANK], BF16, name="rbf_half"))
-            nc.sync.dma_start(rbf_half[h][:], rbf_by_half[:, h])
+        rbf_sb = []
+        for n in range(NEIGHBOURS):
+            rbf_sb.append(per_neighbour.tile([P, ATOMS], BF16, name="rbf_sb"))
+            nc.sync.dma_start(rbf_sb[n][:], rbf[:, n * ATOMS : (n + 1) * ATOMS])
 
         identity = held.tile([P, P], F32, name="identity")
         make_identity(nc, identity[:])
@@ -58,25 +59,23 @@ def tile_spookylocalblock_kernel(tc, atom_fea, w1, b1, wenv, rbf, offs, out):
             nc.tensor.matmul(t_ps[:], w1_sb[:], act[:], start=True, stop=True)
             nc.vector.tensor_scalar(t[:, h * BANK : (h + 1) * BANK], t_ps[:], b1_sb[:, 0:1], None, ADD)
 
-        env = {}
-        for h in range(HALVES):
-            for n in range(NEIGHBOURS):
-                env_ps = banks.tile([P, BANK], F32, name="env_ps", tag="bank")
-                nc.tensor.matmul(env_ps[:], wenv_sb[:], rbf_half[h][:, n, :], start=True, stop=True)
-                env[h, n] = per_piece.tile([P, BANK], F32, name="env_piece")
-                nc.scalar.copy(env[h, n][:], env_ps[:])
+        env = []
+        for k in range(PIECES):
+            n, h = divmod(k, HALVES)
+            env_ps = banks.tile([P, BANK], F32, name="env_ps", tag="bank")
+            nc.tensor.matmul(env_ps[:], wenv_sb[:], rbf_sb[n][:, h * BANK : (h + 1) * BANK], start=True, stop=True)
+            env.append(per_piece.tile([P, BANK], F32, name="env_piece"))
+            nc.scalar.copy(env[k][:], env_ps[:])
 
-        for h in range(HALVES):
-            on_tensor = NEIGHBOURS - 1
-            out_ps = out_banks.tile([P, BANK], F32, name="out_ps")
-            out_sb = per_half.tile([P, BANK], F32, name="out_sb")
-            for n in range(NEIGHBOURS):
-                k = n * HALVES + h
-                prod = per_piece.tile([P, BANK], F32, name="prod")
-                picked = t[:].indirect(offsets[:, k * OFFSET_COLUMNS : (k + 1) * OFFSET_COLUMNS])
-                nc.vector.tensor_tensor(prod[:], picked, env[h, n][:], MULT)
-                if n < on_tensor:
-                    nc.tensor.matmul(out_ps[:], identity[:], prod[:], start=(n == 0), stop=(n == on_tensor - 1))
-                else:
-                    nc.vector.tensor_tensor(out_sb[:], out_ps[:], prod[:], ADD)
-            nc.sync.dma_start(out[:, h * BANK : (h + 1) * BANK], out_sb[:])
+        out_ps = [out_banks.tile([P, BANK], F32, name="out_ps") for h in range(HALVES)]
+        for k in range(PIECES):
+            n, h = divmod(k, HALVES)
+            prod = per_piece.tile([P, BANK], F32, name="prod")
+            picked = t[:].indirect(offsets[:, k * OFFSET_COLUMNS : (k + 1) * OFFSET_COLUMNS])
+            nc.vector.tensor_tensor(prod[:], picked, env[k][:], MULT)
+            if n < NEIGHBOURS - 1:
+                nc.tensor.matmul(out_ps[h][:], identity[:], prod[:], start=(n == 0), stop=(n == NEIGHBOURS - 2))
+            else:
+                out_sb = per_half.tile([P, BANK], F32, name="out_sb")
+                nc.vector.tensor_tensor(out_sb[:], out_ps[h][:], prod[:], ADD)
+                nc.sync.dma_start(out[:, h * BANK : (h + 1) * BANK], out_sb[:])

@@ -17,6 +17,7 @@ HALVES = ATOMS // BANK
 PIECES = ENTRIES // BANK
 PSUM_BANKS = 8
 OFFSET_COLUMNS = BANK // 16
+WARM_UP_MATMULS = 4
 
 FLOPS = 2 * P * P * ATOMS + 2 * P * P * ENTRIES
 
@@ -50,6 +51,10 @@ def tile_spookylocalblock_kernel(tc, atom_fea, w1, b1, wenv, rbf, offs, out):
 
         identity = held.tile([P, P], F32, name="identity")
         make_identity(nc, identity[:])
+
+        warm_ps = banks.tile([P, P], F32, name="warm_ps", tag="bank")
+        for repeat in range(WARM_UP_MATMULS):
+            nc.tensor.matmul(warm_ps[:], identity[:], identity[:], start=True, stop=True)
 
         t = held.tile([P, ATOMS], F32, name="t")
         for h in range(HALVES):

@@ -18,6 +18,8 @@ PIECES = ENTRIES // BANK
 PSUM_BANKS = 8
 OFFSET_COLUMNS = BANK // 16
 WARM_UP_MATMULS = 4
+CHUNK = 256
+CHUNKS = ATOMS // CHUNK
 
 FLOPS = 2 * P * P * ATOMS + 2 * P * P * ENTRIES
 
@@ -27,7 +29,7 @@ def tile_spookylocalblock_kernel(tc, atom_fea, w1, b1, wenv, rbf, offs, out):
     with (
         tc.tile_pool(name="held", bufs=1) as held,
         tc.tile_pool(name="per_half", bufs=HALVES) as per_half,
-        tc.tile_pool(name="per_neighbour", bufs=NEIGHBOURS) as per_neighbour,
+        tc.tile_pool(name="per_chunk", bufs=CHUNKS) as per_chunk,
         tc.tile_pool(name="per_piece", bufs=PIECES) as per_piece,
         tc.psum_pool(name="out_banks", bufs=HALVES) as out_banks,
         tc.psum_pool(name="banks", bufs=PSUM_BANKS - HALVES) as banks,
@@ -43,11 +45,12 @@ def tile_spookylocalblock_kernel(tc, atom_fea, w1, b1, wenv, rbf, offs, out):
         wenv_sb = held.tile([P, P], BF16, name="wenv_sb")
         nc.sync.dma_start(wenv_sb[:], wenv)
         offsets = held.tile([P, ENTRIES // 16], U16, name="offsets")
-        nc.sync.dma_start(offsets[:], offs)
         rbf_sb = []
-        for n in range(NEIGHBOURS):
-            rbf_sb.append(per_neighbour.tile([P, ATOMS], BF16, name="rbf_sb"))
-            nc.sync.dma_start(rbf_sb[n][:], rbf[:, n * ATOMS : (n + 1) * ATOMS])
+        for k in range(PIECES):
+            rbf_sb.append(per_piece.tile([P, BANK], BF16, name="rbf_sb"))
+            nc.sync.dma_start(rbf_sb[k][:], rbf[:, k * BANK : (k + 1) * BANK])
+            if k == 0:
+                nc.sync.dma_start(offsets[:], offs)
 
         identity = held.tile([P, P], F32, name="identity")
         make_identity(nc, identity[:])
@@ -56,21 +59,28 @@ def tile_spookylocalblock_kernel(tc, atom_fea, w1, b1, wenv, rbf, offs, out):
         for repeat in range(WARM_UP_MATMULS):
             nc.tensor.matmul(warm_ps[:], identity[:], identity[:], start=True, stop=True)
 
-        t = held.tile([P, ATOMS], F32, name="t")
-        for h in range(HALVES):
-            act = per_half.tile([P, BANK], BF16, name="act")
-            nc.scalar.activation(act[:], fea[h][:], SILU)
-            t_ps = banks.tile([P, BANK], F32, name="t_ps", tag="bank")
-            nc.tensor.matmul(t_ps[:], w1_sb[:], act[:], start=True, stop=True)
-            nc.vector.tensor_scalar(t[:, h * BANK : (h + 1) * BANK], t_ps[:], b1_sb[:, 0:1], None, ADD)
-
         env = []
-        for k in range(PIECES):
-            n, h = divmod(k, HALVES)
+
+        def make_env_piece(k):
             env_ps = banks.tile([P, BANK], F32, name="env_ps", tag="bank")
-            nc.tensor.matmul(env_ps[:], wenv_sb[:], rbf_sb[n][:, h * BANK : (h + 1) * BANK], start=True, stop=True)
+            nc.tensor.matmul(env_ps[:], wenv_sb[:], rbf_sb[k][:], start=True, stop=True)
             env.append(per_piece.tile([P, BANK], F32, name="env_piece"))
             nc.scalar.copy(env[k][:], env_ps[:])
+
+        act = []
+        for c in range(CHUNKS):
+            h, part = divmod(c, CHUNKS // HALVES)
+            act.append(per_chunk.tile([P, CHUNK], BF16, name="act"))
+            nc.scalar.activation(act[c][:], fea[h][:, part * CHUNK : (part + 1) * CHUNK], SILU)
+        t = held.tile([P, ATOMS], F32, name="t")
+        for c in range(CHUNKS):
+            t_ps = banks.tile([P, CHUNK], F32, name="t_ps", tag="bank")
+            nc.tensor.matmul(t_ps[:], w1_sb[:], act[c][:], start=True, stop=True)
+            nc.vector.tensor_scalar(t[:, c * CHUNK : (c + 1) * CHUNK], t_ps[:], b1_sb[:, 0:1], None, ADD)
+            if c == CHUNKS - 2:
+                make_env_piece(0)
+        for k in range(1, PIECES):
+            make_env_piece(k)
 
         out_ps = [out_banks.tile([P, BANK], F32, name="out_ps") for h in range(HALVES)]
         for k in range(PIECES):

@@ -26,6 +26,11 @@ FLOPS = 2 * P * P * ATOMS + 2 * P * P * ENTRIES
 
 def tile_spookylocalblock_kernel(tc, atom_fea, w1, b1, wenv, rbf, offs, out):
     nc = tc.nc
+
+    def first_entry(k):
+        h, n = divmod(k, NEIGHBOURS)
+        return n * ATOMS + h * BANK
+
     with (
         tc.tile_pool(name="held", bufs=1) as held,
         tc.tile_pool(name="per_half", bufs=HALVES) as per_half,
@@ -48,7 +53,7 @@ def tile_spookylocalblock_kernel(tc, atom_fea, w1, b1, wenv, rbf, offs, out):
         rbf_sb = []
         for k in range(PIECES):
             rbf_sb.append(per_piece.tile([P, BANK], BF16, name="rbf_sb"))
-            nc.sync.dma_start(rbf_sb[k][:], rbf[:, k * BANK : (k + 1) * BANK])
+            nc.sync.dma_start(rbf_sb[k][:], rbf[:, first_entry(k) : first_entry(k) + BANK])
             if k == 0:
                 nc.sync.dma_start(offsets[:], offs)
 
@@ -84,13 +89,18 @@ def tile_spookylocalblock_kernel(tc, atom_fea, w1, b1, wenv, rbf, offs, out):
 
         out_ps = [out_banks.tile([P, BANK], F32, name="out_ps") for h in range(HALVES)]
         for k in range(PIECES):
-            n, h = divmod(k, HALVES)
+            h, n = divmod(k, NEIGHBOURS)
+            first_column = first_entry(k) // 16
             prod = per_piece.tile([P, BANK], F32, name="prod")
-            picked = t[:].indirect(offsets[:, k * OFFSET_COLUMNS : (k + 1) * OFFSET_COLUMNS])
+            picked = t[:].indirect(offsets[:, first_column : first_column + OFFSET_COLUMNS])
             nc.vector.tensor_tensor(prod[:], picked, env[k][:], MULT)
-            if n < NEIGHBOURS - 1:
-                nc.tensor.matmul(out_ps[h][:], identity[:], prod[:], start=(n == 0), stop=(n == NEIGHBOURS - 2))
-            else:
+            if k < PIECES - 1:
+                closes = n == NEIGHBOURS - 1 or k == PIECES - 2
+                nc.tensor.matmul(out_ps[h][:], identity[:], prod[:], start=(n == 0), stop=closes)
+            if n == NEIGHBOURS - 1:
                 out_sb = per_half.tile([P, BANK], F32, name="out_sb")
-                nc.vector.tensor_tensor(out_sb[:], out_ps[h][:], prod[:], ADD)
+                if k < PIECES - 1:
+                    nc.scalar.copy(out_sb[:], out_ps[h][:])
+                else:
+                    nc.vector.tensor_tensor(out_sb[:], out_ps[h][:], prod[:], ADD)
                 nc.sync.dma_start(out[:, h * BANK : (h + 1) * BANK], out_sb[:])

@@ -18,6 +18,8 @@ PIECES = ENTRIES // BANK
 PSUM_BANKS = 8
 OFFSET_COLUMNS = BANK // 16
 WARM_UP_MATMULS = 4
+LAST_HALF_GROUPS = 2
+OUT_BANKS = HALVES - 1 + LAST_HALF_GROUPS
 CHUNK = 256
 CHUNKS = ATOMS // CHUNK
 
@@ -36,8 +38,8 @@ def tile_spookylocalblock_kernel(tc, atom_fea, w1, b1, wenv, rbf, offs, out):
         tc.tile_pool(name="per_half", bufs=HALVES) as per_half,
         tc.tile_pool(name="per_chunk", bufs=CHUNKS) as per_chunk,
         tc.tile_pool(name="per_piece", bufs=PIECES) as per_piece,
-        tc.psum_pool(name="out_banks", bufs=HALVES) as out_banks,
-        tc.psum_pool(name="banks", bufs=PSUM_BANKS - HALVES) as banks,
+        tc.psum_pool(name="out_banks", bufs=OUT_BANKS) as out_banks,
+        tc.psum_pool(name="banks", bufs=PSUM_BANKS - OUT_BANKS) as banks,
     ):
         fea = []
         for h in range(HALVES):
@@ -87,20 +89,27 @@ def tile_spookylocalblock_kernel(tc, atom_fea, w1, b1, wenv, rbf, offs, out):
         for k in range(1, PIECES):
             make_env_piece(k)
 
-        out_ps = [out_banks.tile([P, BANK], F32, name="out_ps") for h in range(HALVES)]
+        def groups_of(h):
+            count = LAST_HALF_GROUPS if h == HALVES - 1 else 1
+            return [(g * (BANK // count), BANK // count) for g in range(count)]
+
+        out_ps = [[out_banks.tile([P, BANK], F32, name="out_ps") for group in groups_of(h)] for h in range(HALVES)]
         for k in range(PIECES):
             h, n = divmod(k, NEIGHBOURS)
             first_column = first_entry(k) // 16
             prod = per_piece.tile([P, BANK], F32, name="prod")
             picked = t[:].indirect(offsets[:, first_column : first_column + OFFSET_COLUMNS])
             nc.vector.tensor_tensor(prod[:], picked, env[k][:], MULT)
-            if k < PIECES - 1:
-                closes = n == NEIGHBOURS - 1 or k == PIECES - 2
-                nc.tensor.matmul(out_ps[h][:], identity[:], prod[:], start=(n == 0), stop=closes)
             if n == NEIGHBOURS - 1:
                 out_sb = per_half.tile([P, BANK], F32, name="out_sb")
+            for g, (first, width) in enumerate(groups_of(h)):
+                group_ps = out_ps[h][g][:, :width]
                 if k < PIECES - 1:
-                    nc.scalar.copy(out_sb[:], out_ps[h][:])
-                else:
-                    nc.vector.tensor_tensor(out_sb[:], out_ps[h][:], prod[:], ADD)
-                nc.sync.dma_start(out[:, h * BANK : (h + 1) * BANK], out_sb[:])
+                    closes = n == NEIGHBOURS - 1 or k == PIECES - 2
+                    nc.tensor.matmul(group_ps, identity[:], prod[:, first : first + width], start=(n == 0), stop=closes)
+                if n == NEIGHBOURS - 1:
+                    if k < PIECES - 1:
+                        nc.scalar.copy(out_sb[:, first : first + width], group_ps)
+                    else:
+                        nc.vector.tensor_tensor(out_sb[:, first : first + width], group_ps, prod[:, first : first + width], ADD)
+                    nc.sync.dma_start(out[:, h * BANK + first : h * BANK + first + width], out_sb[:, first : first + width])

@@ -112,4 +112,5 @@ def tile_spookylocalblock_kernel(tc, atom_fea, w1, b1, wenv, rbf, offs, out):
                         nc.scalar.copy(out_sb[:, first : first + width], group_ps)
                     else:
                         nc.vector.tensor_tensor(out_sb[:, first : first + width], group_ps, prod[:, first : first + width], ADD)
-                    nc.sync.dma_start(out[:, h * BANK + first : h * BANK + first + width], out_sb[:, first : first + width])
+            if n == NEIGHBOURS - 1:
+                nc.sync.dma_start(out[:, h * BANK : (h + 1) * BANK], out_sb[:])

@@ -16,10 +16,8 @@ BANK = 512
 HALVES = ATOMS // BANK
 PIECES = ENTRIES // BANK
 PSUM_BANKS = 8
-OFFSET_COLUMNS = BANK // 16
 WARM_UP_MATMULS = 4
 LAST_HALF_GROUPS = 2
-OUT_BANKS = HALVES - 1 + LAST_HALF_GROUPS
 CHUNK = 256
 CHUNKS = ATOMS // CHUNK
 
@@ -38,8 +36,7 @@ def tile_spookylocalblock_kernel(tc, atom_fea, w1, b1, wenv, rbf, offs, out):
         tc.tile_pool(name="per_half", bufs=HALVES) as per_half,
         tc.tile_pool(name="per_chunk", bufs=CHUNKS) as per_chunk,
         tc.tile_pool(name="per_piece", bufs=PIECES) as per_piece,
-        tc.psum_pool(name="out_banks", bufs=OUT_BANKS) as out_banks,
-        tc.psum_pool(name="banks", bufs=PSUM_BANKS - OUT_BANKS) as banks,
+        tc.psum_pool(name="banks", bufs=PSUM_BANKS) as banks,
     ):
         fea = []
         for h in range(HALVES):
@@ -93,17 +90,20 @@ def tile_spookylocalblock_kernel(tc, atom_fea, w1, b1, wenv, rbf, offs, out):
             count = LAST_HALF_GROUPS if h == HALVES - 1 else 1
             return [(g * (BANK // count), BANK // count) for g in range(count)]
 
-        out_ps = [[out_banks.tile([P, BANK], F32, name="out_ps") for group in groups_of(h)] for h in range(HALVES)]
         for k in range(PIECES):
             h, n = divmod(k, NEIGHBOURS)
+            if n == 0:
+                out_ps = [banks.tile([P, BANK], F32, name="out_ps", tag="bank") for group in groups_of(h)]
             first_column = first_entry(k) // 16
             prod = per_piece.tile([P, BANK], F32, name="prod")
-            picked = t[:].indirect(offsets[:, first_column : first_column + OFFSET_COLUMNS])
-            nc.vector.tensor_tensor(prod[:], picked, env[k][:], MULT)
+            for first, width in groups_of(h) if k == PIECES - 1 else [(0, BANK)]:
+                offset = first_column + first // 16
+                picked = t[:].indirect(offsets[:, offset : offset + width // 16])
+                nc.vector.tensor_tensor(prod[:, first : first + width], picked, env[k][:, first : first + width], MULT)
             if n == NEIGHBOURS - 1:
                 out_sb = per_half.tile([P, BANK], F32, name="out_sb")
             for g, (first, width) in enumerate(groups_of(h)):
-                group_ps = out_ps[h][g][:, :width]
+                group_ps = out_ps[g][:, :width]
                 if k < PIECES - 1:
                     closes = n == NEIGHBOURS - 1 or k == PIECES - 2
                     nc.tensor.matmul(group_ps, identity[:], prod[:, first : first + width], start=(n == 0), stop=closes)

@@ -31,6 +31,10 @@ def tile_spookylocalblock_kernel(tc, atom_fea, w1, b1, wenv, rbf, offs, out):
         h, n = divmod(k, NEIGHBOURS)
         return n * ATOMS + h * BANK
 
+    def parts_of(k):
+        width = BANK // 2 if k in (0, PIECES - 1) else BANK
+        return [(first, width) for first in range(0, BANK, width)]
+
     with (
         tc.tile_pool(name="held", bufs=1) as held,
         tc.tile_pool(name="per_half", bufs=HALVES) as per_half,
@@ -38,38 +42,44 @@ def tile_spookylocalblock_kernel(tc, atom_fea, w1, b1, wenv, rbf, offs, out):
         tc.tile_pool(name="per_piece", bufs=PIECES) as per_piece,
         tc.psum_pool(name="banks", bufs=PSUM_BANKS) as banks,
     ):
+        w1_sb = held.tile([P, P], BF16, name="w1_sb")
+        b1_sb = held.tile([P, 1], F32, name="b1_sb")
         fea = []
         for h in range(HALVES):
             fea.append(per_half.tile([P, BANK], F32, name="fea"))
             nc.sync.dma_start(fea[h][:], atom_fea[:, h * BANK : (h + 1) * BANK])
-        w1_sb = held.tile([P, P], BF16, name="w1_sb")
-        nc.sync.dma_start(w1_sb[:], w1)
-        b1_sb = held.tile([P, 1], F32, name="b1_sb")
-        nc.sync.dma_start(b1_sb[:], b1)
+            if h == 0:
+                nc.sync.dma_start(w1_sb[:], w1)
+                nc.sync.dma_start(b1_sb[:], b1)
         wenv_sb = held.tile([P, P], BF16, name="wenv_sb")
         nc.sync.dma_start(wenv_sb[:], wenv)
         offsets = held.tile([P, ENTRIES // 16], U16, name="offsets")
         rbf_sb = []
         for k in range(PIECES):
             rbf_sb.append(per_piece.tile([P, BANK], BF16, name="rbf_sb"))
-            nc.sync.dma_start(rbf_sb[k][:], rbf[:, first_entry(k) : first_entry(k) + BANK])
-            if k == 0:
-                nc.sync.dma_start(offsets[:], offs)
+            for first, width in parts_of(k):
+                entry = first_entry(k) + first
+                nc.sync.dma_start(rbf_sb[k][:, first : first + width], rbf[:, entry : entry + width])
+                if k == 0 and first == 0:
+                    nc.sync.dma_start(offsets[:], offs)
 
+        zeros = held.tile([P, P], F32, name="zeros")
+        nc.vector.memset(zeros[:], 0.0)
         identity = held.tile([P, P], F32, name="identity")
         make_identity(nc, identity[:])
 
         warm_ps = banks.tile([P, P], F32, name="warm_ps", tag="bank")
         for repeat in range(WARM_UP_MATMULS):
-            nc.tensor.matmul(warm_ps[:], identity[:], identity[:], start=True, stop=True)
+            nc.tensor.matmul(warm_ps[:], zeros[:], zeros[:], start=True, stop=True)
 
         env = []
 
-        def make_env_piece(k):
+        def make_env_part(k, first, width):
+            if first == 0:
+                env.append(per_piece.tile([P, BANK], F32, name="env_piece"))
             env_ps = banks.tile([P, BANK], F32, name="env_ps", tag="bank")
-            nc.tensor.matmul(env_ps[:], wenv_sb[:], rbf_sb[k][:], start=True, stop=True)
-            env.append(per_piece.tile([P, BANK], F32, name="env_piece"))
-            nc.scalar.copy(env[k][:], env_ps[:])
+            nc.tensor.matmul(env_ps[:, :width], wenv_sb[:], rbf_sb[k][:, first : first + width], start=True, stop=True)
+            nc.scalar.copy(env[k][:, first : first + width], env_ps[:, :width])
 
         act = []
         for c in range(CHUNKS):
@@ -78,13 +88,15 @@ def tile_spookylocalblock_kernel(tc, atom_fea, w1, b1, wenv, rbf, offs, out):
             nc.scalar.activation(act[c][:], fea[h][:, part * CHUNK : (part + 1) * CHUNK], SILU)
         t = held.tile([P, ATOMS], F32, name="t")
         for c in range(CHUNKS):
+            if c == CHUNKS - 1:
+                make_env_part(0, *parts_of(0)[0])
             t_ps = banks.tile([P, CHUNK], F32, name="t_ps", tag="bank")
             nc.tensor.matmul(t_ps[:], w1_sb[:], act[c][:], start=True, stop=True)
             nc.vector.tensor_scalar(t[:, c * CHUNK : (c + 1) * CHUNK], t_ps[:], b1_sb[:, 0:1], None, ADD)
-            if c == CHUNKS - 2:
-                make_env_piece(0)
-        for k in range(1, PIECES):
-            make_env_piece(k)
+        for k in range(PIECES):
+            for first, width in parts_of(k):
+                if k > 0 or first > 0:
+                    make_env_part(k, first, width)
 
         def groups_of(h):
             count = LAST_HALF_GROUPS if h == HALVES - 1 else 1
@@ -96,7 +108,7 @@ def tile_spookylocalblock_kernel(tc, atom_fea, w1, b1, wenv, rbf, offs, out):
                 out_ps = [banks.tile([P, BANK], F32, name="out_ps", tag="bank") for group in groups_of(h)]
             first_column = first_entry(k) // 16
             prod = per_piece.tile([P, BANK], F32, name="prod")
-            for first, width in groups_of(h) if k == PIECES - 1 else [(0, BANK)]:
+            for first, width in parts_of(k):
                 offset = first_column + first // 16
                 picked = t[:].indirect(offsets[:, offset : offset + width // 16])
                 nc.vector.tensor_tensor(prod[:, first : first + width], picked, env[k][:, first : first + width], MULT)

@@ -16,7 +16,7 @@ BANK = 512
 HALVES = ATOMS // BANK
 PIECES = ENTRIES // BANK
 PSUM_BANKS = 8
-WARM_UP_MATMULS = 4
+WARM_UP_MATMULS = 3
 LAST_HALF_GROUPS = 2
 CHUNK = 256
 CHUNKS = ATOMS // CHUNK
@@ -32,7 +32,7 @@ def tile_spookylocalblock_kernel(tc, atom_fea, w1, b1, wenv, rbf, offs, out):
         return n * ATOMS + h * BANK
 
     def parts_of(k):
-        width = BANK // 2 if k in (0, PIECES - 1) else BANK
+        width = BANK // 2 if k == 0 or k >= PIECES - 2 else BANK
         return [(first, width) for first in range(0, BANK, width)]
 
     with (
@@ -45,23 +45,25 @@ def tile_spookylocalblock_kernel(tc, atom_fea, w1, b1, wenv, rbf, offs, out):
         w1_sb = held.tile([P, P], BF16, name="w1_sb")
         b1_sb = held.tile([P, 1], F32, name="b1_sb")
         fea = []
-        for h in range(HALVES):
-            fea.append(per_half.tile([P, BANK], F32, name="fea"))
-            nc.sync.dma_start(fea[h][:], atom_fea[:, h * BANK : (h + 1) * BANK])
-            if h == 0:
+        for c in range(CHUNKS):
+            fea.append(per_chunk.tile([P, CHUNK], F32, name="fea"))
+            nc.sync.dma_start(fea[c][:], atom_fea[:, c * CHUNK : (c + 1) * CHUNK])
+            if c == 0:
                 nc.sync.dma_start(w1_sb[:], w1)
                 nc.sync.dma_start(b1_sb[:], b1)
         wenv_sb = held.tile([P, P], BF16, name="wenv_sb")
         nc.sync.dma_start(wenv_sb[:], wenv)
         offsets = held.tile([P, ENTRIES // 16], U16, name="offsets")
-        rbf_sb = []
-        for k in range(PIECES):
-            rbf_sb.append(per_piece.tile([P, BANK], BF16, name="rbf_sb"))
-            for first, width in parts_of(k):
-                entry = first_entry(k) + first
-                nc.sync.dma_start(rbf_sb[k][:, first : first + width], rbf[:, entry : entry + width])
-                if k == 0 and first == 0:
-                    nc.sync.dma_start(offsets[:], offs)
+        rbf_all = held.tile([P, PIECES, BANK], BF16, name="rbf_all")
+        by_half = rbf.rearrange("q (n h a) -> q h n a", n=NEIGHBOURS, h=HALVES)
+        for first, width in parts_of(0):
+            nc.sync.dma_start(rbf_all[:, 0, first : first + width], by_half[:, 0, 0, first : first + width])
+            if first == 0:
+                nc.sync.dma_start(offsets[:], offs)
+        nc.sync.dma_start(rbf_all[:, 1, :], by_half[:, 0, 1, :])
+        for k in range(2, PIECES, 2):
+            h, n = divmod(k, NEIGHBOURS)
+            nc.sync.dma_start(rbf_all[:, k : k + 2, :], by_half[:, h, n : n + 2, :])
 
         zeros = held.tile([P, P], F32, name="zeros")
         nc.vector.memset(zeros[:], 0.0)
@@ -78,25 +80,21 @@ def tile_spookylocalblock_kernel(tc, atom_fea, w1, b1, wenv, rbf, offs, out):
             if first == 0:
                 env.append(per_piece.tile([P, BANK], F32, name="env_piece"))
             env_ps = banks.tile([P, BANK], F32, name="env_ps", tag="bank")
-            nc.tensor.matmul(env_ps[:, :width], wenv_sb[:], rbf_sb[k][:, first : first + width], start=True, stop=True)
+            nc.tensor.matmul(env_ps[:, :width], wenv_sb[:], rbf_all[:, k, first : first + width], start=True, stop=True)
             nc.scalar.copy(env[k][:, first : first + width], env_ps[:, :width])
 
         act = []
         for c in range(CHUNKS):
-            h, part = divmod(c, CHUNKS // HALVES)
             act.append(per_chunk.tile([P, CHUNK], BF16, name="act"))
-            nc.scalar.activation(act[c][:], fea[h][:, part * CHUNK : (part + 1) * CHUNK], SILU)
+            nc.scalar.activation(act[c][:], fea[c][:], SILU)
         t = held.tile([P, ATOMS], F32, name="t")
         for c in range(CHUNKS):
-            if c == CHUNKS - 1:
-                make_env_part(0, *parts_of(0)[0])
             t_ps = banks.tile([P, CHUNK], F32, name="t_ps", tag="bank")
             nc.tensor.matmul(t_ps[:], w1_sb[:], act[c][:], start=True, stop=True)
             nc.vector.tensor_scalar(t[:, c * CHUNK : (c + 1) * CHUNK], t_ps[:], b1_sb[:, 0:1], None, ADD)
         for k in range(PIECES):
             for first, width in parts_of(k):
-                if k > 0 or first > 0:
-                    make_env_part(k, first, width)
+                make_env_part(k, first, width)
 
         def groups_of(h):
             count = LAST_HALF_GROUPS if h == HALVES - 1 else 1

@@ -56,10 +56,8 @@ def tile_spookylocalblock_kernel(tc, atom_fea, w1, b1, wenv, rbf, offs, out):
         offsets = held.tile([P, ENTRIES // 16], U16, name="offsets")
         rbf_all = held.tile([P, PIECES, BANK], BF16, name="rbf_all")
         by_half = rbf.rearrange("q (n h a) -> q h n a", n=NEIGHBOURS, h=HALVES)
-        for first, width in parts_of(0):
-            nc.sync.dma_start(rbf_all[:, 0, first : first + width], by_half[:, 0, 0, first : first + width])
-            if first == 0:
-                nc.sync.dma_start(offsets[:], offs)
+        nc.sync.dma_start(rbf_all[:, 0, :], by_half[:, 0, 0, :])
+        nc.sync.dma_start(offsets[:], offs)
         nc.sync.dma_start(rbf_all[:, 1, :], by_half[:, 0, 1, :])
         for k in range(2, PIECES, 2):
             h, n = divmod(k, NEIGHBOURS)
@@ -122,5 +120,5 @@ def tile_spookylocalblock_kernel(tc, atom_fea, w1, b1, wenv, rbf, offs, out):
                         nc.scalar.copy(out_sb[:, first : first + width], group_ps)
                     else:
                         nc.vector.tensor_tensor(out_sb[:, first : first + width], group_ps, prod[:, first : first + width], ADD)
-            if n == NEIGHBOURS - 1:
-                nc.sync.dma_start(out[:, h * BANK : (h + 1) * BANK], out_sb[:])
+                    atom = h * BANK + first
+                    nc.sync.dma_start(out[:, atom : atom + width], out_sb[:, first : first + width])

@@ -17,7 +17,8 @@ HALVES = ATOMS // BANK
 PIECES = ENTRIES // BANK
 PSUM_BANKS = 8
 WARM_UP_MATMULS = 3
-LAST_HALF_GROUPS = 2
+FIRST_PARTS = [BANK // 2, BANK // 2]
+LAST_GROUPS = [320, 192]
 CHUNK = 256
 CHUNKS = ATOMS // CHUNK
 
@@ -32,8 +33,8 @@ def tile_spookylocalblock_kernel(tc, atom_fea, w1, b1, wenv, rbf, offs, out):
         return n * ATOMS + h * BANK
 
     def parts_of(k):
-        width = BANK // 2 if k == 0 or k >= PIECES - 2 else BANK
-        return [(first, width) for first in range(0, BANK, width)]
+        widths = FIRST_PARTS if k == 0 else LAST_GROUPS if k >= PIECES - 2 else [BANK]
+        return [(sum(widths[:i]), width) for i, width in enumerate(widths)]
 
     with (
         tc.tile_pool(name="held", bufs=1) as held,
@@ -50,7 +51,7 @@ def tile_spookylocalblock_kernel(tc, atom_fea, w1, b1, wenv, rbf, offs, out):
             nc.sync.dma_start(fea[c][:], atom_fea[:, c * CHUNK : (c + 1) * CHUNK])
             if c == 0:
                 nc.sync.dma_start(w1_sb[:], w1)
-                nc.sync.dma_start(b1_sb[:], b1)
+        nc.sync.dma_start(b1_sb[:], b1)
         wenv_sb = held.tile([P, P], BF16, name="wenv_sb")
         nc.sync.dma_start(wenv_sb[:], wenv)
         offsets = held.tile([P, ENTRIES // 16], U16, name="offsets")
@@ -95,8 +96,8 @@ def tile_spookylocalblock_kernel(tc, atom_fea, w1, b1, wenv, rbf, offs, out):
                 make_env_part(k, first, width)
 
         def groups_of(h):
-            count = LAST_HALF_GROUPS if h == HALVES - 1 else 1
-            return [(g * (BANK // count), BANK // count) for g in range(count)]
+            widths = LAST_GROUPS if h == HALVES - 1 else [BANK]
+            return [(sum(widths[:i]), width) for i, width in enumerate(widths)]
 
         for k in range(PIECES):
             h, n = divmod(k, NEIGHBOURS)

@@ -7,6 +7,7 @@ U16 = mybir.dt.uint16
 MULT = mybir.AluOpType.mult
 ADD = mybir.AluOpType.add
 SILU = mybir.ActivationFunctionType.Silu
+IDENTITY = mybir.ActivationFunctionType.Identity
 
 P = 128
 ATOMS = 1024
@@ -16,25 +17,35 @@ BANK = 512
 HALVES = ATOMS // BANK
 PIECES = ENTRIES // BANK
 PSUM_BANKS = 8
+ENTRIES_PER_OFFSET_COLUMN = 16
 WARM_UP_MATMULS = 3
-FIRST_PARTS = [BANK // 2, BANK // 2]
-LAST_GROUPS = [320, 192]
 CHUNK = 256
 CHUNKS = ATOMS // CHUNK
+LAST_CHUNK_PARTS = [CHUNK // 2, CHUNK // 2]
+
+FIRST_PIECE_PARTS = [192, 320]
+LAST_GROUPS = [320, 192]
+GROUPED_PIECES = 2
 
 FLOPS = 2 * P * P * ATOMS + 2 * P * P * ENTRIES
 
 
+def spans(widths):
+    return [(sum(widths[:i]), width) for i, width in enumerate(widths)]
+
+
+def groups_of(half):
+    return spans(LAST_GROUPS) if half == HALVES - 1 else spans([BANK])
+
+
+def parts_of(k):
+    if k == 0:
+        return spans(FIRST_PIECE_PARTS)
+    return spans(LAST_GROUPS) if k >= PIECES - GROUPED_PIECES else spans([BANK])
+
+
 def tile_spookylocalblock_kernel(tc, atom_fea, w1, b1, wenv, rbf, offs, out):
     nc = tc.nc
-
-    def first_entry(k):
-        h, n = divmod(k, NEIGHBOURS)
-        return n * ATOMS + h * BANK
-
-    def parts_of(k):
-        widths = FIRST_PARTS if k == 0 else LAST_GROUPS if k >= PIECES - 2 else [BANK]
-        return [(sum(widths[:i]), width) for i, width in enumerate(widths)]
 
     with (
         tc.tile_pool(name="held", bufs=1) as held,
@@ -44,82 +55,75 @@ def tile_spookylocalblock_kernel(tc, atom_fea, w1, b1, wenv, rbf, offs, out):
         tc.psum_pool(name="banks", bufs=PSUM_BANKS) as banks,
     ):
         w1_sb = held.tile([P, P], BF16, name="w1_sb")
-        b1_sb = held.tile([P, 1], F32, name="b1_sb")
         fea = []
         for c in range(CHUNKS):
             fea.append(per_chunk.tile([P, CHUNK], F32, name="fea"))
             nc.sync.dma_start(fea[c][:], atom_fea[:, c * CHUNK : (c + 1) * CHUNK])
             if c == 0:
                 nc.sync.dma_start(w1_sb[:], w1)
+        b1_sb = held.tile([P, 1], F32, name="b1_sb")
         nc.sync.dma_start(b1_sb[:], b1)
         wenv_sb = held.tile([P, P], BF16, name="wenv_sb")
         nc.sync.dma_start(wenv_sb[:], wenv)
-        offsets = held.tile([P, ENTRIES // 16], U16, name="offsets")
-        rbf_all = held.tile([P, PIECES, BANK], BF16, name="rbf_all")
-        by_half = rbf.rearrange("q (n h a) -> q h n a", n=NEIGHBOURS, h=HALVES)
-        nc.sync.dma_start(rbf_all[:, 0, :], by_half[:, 0, 0, :])
+        rbf_sb = held.tile([P, PIECES, BANK], BF16, name="rbf_sb")
+        rbf_pieces = rbf.rearrange("q (n h a) -> q h n a", n=NEIGHBOURS, h=HALVES)
+        offsets = held.tile([P, ENTRIES // ENTRIES_PER_OFFSET_COLUMN], U16, name="offsets")
+        nc.sync.dma_start(rbf_sb[:, 0, :], rbf_pieces[:, 0, 0, :])
         nc.sync.dma_start(offsets[:], offs)
-        nc.sync.dma_start(rbf_all[:, 1, :], by_half[:, 0, 1, :])
+        nc.sync.dma_start(rbf_sb[:, 1, :], rbf_pieces[:, 0, 1, :])
         for k in range(2, PIECES, 2):
             h, n = divmod(k, NEIGHBOURS)
-            nc.sync.dma_start(rbf_all[:, k : k + 2, :], by_half[:, h, n : n + 2, :])
+            nc.sync.dma_start(rbf_sb[:, k : k + 2, :], rbf_pieces[:, h, n : n + 2, :])
 
-        zeros = held.tile([P, P], F32, name="zeros")
-        nc.vector.memset(zeros[:], 0.0)
         identity = held.tile([P, P], F32, name="identity")
         make_identity(nc, identity[:])
 
         warm_ps = banks.tile([P, P], F32, name="warm_ps", tag="bank")
         for repeat in range(WARM_UP_MATMULS):
-            nc.tensor.matmul(warm_ps[:], zeros[:], zeros[:], start=True, stop=True)
+            nc.tensor.matmul(warm_ps[:], identity[:], identity[:], start=True, stop=True)
 
-        env = []
-
-        def make_env_part(k, first, width):
-            if first == 0:
-                env.append(per_piece.tile([P, BANK], F32, name="env_piece"))
-            env_ps = banks.tile([P, BANK], F32, name="env_ps", tag="bank")
-            nc.tensor.matmul(env_ps[:, :width], wenv_sb[:], rbf_all[:, k, first : first + width], start=True, stop=True)
-            nc.scalar.copy(env[k][:, first : first + width], env_ps[:, :width])
-
-        act = []
-        for c in range(CHUNKS):
-            act.append(per_chunk.tile([P, CHUNK], BF16, name="act"))
-            nc.scalar.activation(act[c][:], fea[c][:], SILU)
         t = held.tile([P, ATOMS], F32, name="t")
         for c in range(CHUNKS):
-            t_ps = banks.tile([P, CHUNK], F32, name="t_ps", tag="bank")
-            nc.tensor.matmul(t_ps[:], w1_sb[:], act[c][:], start=True, stop=True)
-            nc.vector.tensor_scalar(t[:, c * CHUNK : (c + 1) * CHUNK], t_ps[:], b1_sb[:, 0:1], None, ADD)
-        for k in range(PIECES):
-            for first, width in parts_of(k):
-                make_env_part(k, first, width)
+            act = per_chunk.tile([P, CHUNK], BF16, name="act")
+            nc.scalar.activation(act[:], fea[c][:], SILU)
+            for first, width in spans([CHUNK]) if c < CHUNKS - 1 else spans(LAST_CHUNK_PARTS):
+                t_ps = banks.tile([P, CHUNK], F32, name="t_ps", tag="bank")
+                nc.tensor.matmul(t_ps[:, :width], w1_sb[:], act[:, first : first + width], start=True, stop=True)
+                t_part = t[:, c * CHUNK + first : c * CHUNK + first + width]
+                if first == 0:
+                    nc.vector.tensor_scalar(t_part, t_ps[:, :width], b1_sb[:, 0:1], None, ADD)
+                else:
+                    nc.scalar.activation(t_part, t_ps[:, :width], IDENTITY, bias=b1_sb[:, 0:1])
 
-        def groups_of(h):
-            widths = LAST_GROUPS if h == HALVES - 1 else [BANK]
-            return [(sum(widths[:i]), width) for i, width in enumerate(widths)]
+        env = []
+        for k in range(PIECES):
+            env.append(per_piece.tile([P, BANK], F32, name="env"))
+            for first, width in parts_of(k):
+                env_ps = banks.tile([P, BANK], F32, name="env_ps", tag="bank")
+                nc.tensor.matmul(env_ps[:, :width], wenv_sb[:], rbf_sb[:, k, first : first + width], start=True, stop=True)
+                nc.scalar.copy(env[k][:, first : first + width], env_ps[:, :width])
 
         for k in range(PIECES):
             h, n = divmod(k, NEIGHBOURS)
             if n == 0:
-                out_ps = [banks.tile([P, BANK], F32, name="out_ps", tag="bank") for group in groups_of(h)]
-            first_column = first_entry(k) // 16
+                sums = [banks.tile([P, BANK], F32, name="sums", tag="bank") for group in groups_of(h)]
+                out_sb = per_half.tile([P, BANK], F32, name="out_sb")
             prod = per_piece.tile([P, BANK], F32, name="prod")
             for first, width in parts_of(k):
-                offset = first_column + first // 16
-                picked = t[:].indirect(offsets[:, offset : offset + width // 16])
+                column = (n * ATOMS + h * BANK + first) // ENTRIES_PER_OFFSET_COLUMN
+                picked = t[:].indirect(offsets[:, column : column + width // ENTRIES_PER_OFFSET_COLUMN])
                 nc.vector.tensor_tensor(prod[:, first : first + width], picked, env[k][:, first : first + width], MULT)
-            if n == NEIGHBOURS - 1:
-                out_sb = per_half.tile([P, BANK], F32, name="out_sb")
             for g, (first, width) in enumerate(groups_of(h)):
-                group_ps = out_ps[g][:, :width]
+                group_sum = sums[g][:, :width]
+                group_prod = prod[:, first : first + width]
+                group_out = out_sb[:, first : first + width]
                 if k < PIECES - 1:
                     closes = n == NEIGHBOURS - 1 or k == PIECES - 2
-                    nc.tensor.matmul(group_ps, identity[:], prod[:, first : first + width], start=(n == 0), stop=closes)
+                    nc.tensor.matmul(group_sum, identity[:], group_prod, start=(n == 0), stop=closes)
                 if n == NEIGHBOURS - 1:
                     if k < PIECES - 1:
-                        nc.scalar.copy(out_sb[:, first : first + width], group_ps)
+                        nc.scalar.copy(group_out, group_sum)
                     else:
-                        nc.vector.tensor_tensor(out_sb[:, first : first + width], group_ps, prod[:, first : first + width], ADD)
+                        nc.vector.tensor_tensor(group_out, group_sum, group_prod, ADD)
                     atom = h * BANK + first
-                    nc.sync.dma_start(out[:, atom : atom + width], out_sb[:, first : first + width])
+                    nc.sync.dma_start(out[:, atom : atom + width], group_out)

import concourse.mybir as mybir
from concourse.masks import make_identity

F32 = mybir.dt.float32
BF16 = mybir.dt.bfloat16
U16 = mybir.dt.uint16
MULT = mybir.AluOpType.mult
ADD = mybir.AluOpType.add
SILU = mybir.ActivationFunctionType.Silu
IDENTITY = mybir.ActivationFunctionType.Identity

P = 128
ATOMS = 1024
NEIGHBOURS = 4
ENTRIES = NEIGHBOURS * ATOMS
BANK = 512
HALVES = ATOMS // BANK
PIECES = ENTRIES // BANK
PSUM_BANKS = 8
ENTRIES_PER_OFFSET_COLUMN = 16
WARM_UP_MATMULS = 3
CHUNK = 256
CHUNKS = ATOMS // CHUNK
LAST_CHUNK_PARTS = [CHUNK // 2, CHUNK // 2]

FIRST_PIECE_PARTS = [192, 320]
LAST_GROUPS = [320, 192]
GROUPED_PIECES = 2

FLOPS = 2 * P * P * ATOMS + 2 * P * P * ENTRIES


def spans(widths):
    return [(sum(widths[:i]), width) for i, width in enumerate(widths)]


def groups_of(half):
    return spans(LAST_GROUPS) if half == HALVES - 1 else spans([BANK])


def parts_of(k):
    if k == 0:
        return spans(FIRST_PIECE_PARTS)
    return spans(LAST_GROUPS) if k >= PIECES - GROUPED_PIECES else spans([BANK])


def tile_spookylocalblock_kernel(tc, atom_fea, w1, b1, wenv, rbf, offs, out):
    nc = tc.nc

    with (
        tc.tile_pool(name="held", bufs=1) as held,
        tc.tile_pool(name="per_half", bufs=HALVES) as per_half,
        tc.tile_pool(name="per_chunk", bufs=CHUNKS) as per_chunk,
        tc.tile_pool(name="per_piece", bufs=PIECES) as per_piece,
        tc.psum_pool(name="banks", bufs=PSUM_BANKS) as banks,
    ):
        w1_sb = held.tile([P, P], BF16, name="w1_sb")
        fea = []
        for c in range(CHUNKS):
            fea.append(per_chunk.tile([P, CHUNK], F32, name="fea"))
            nc.sync.dma_start(fea[c][:], atom_fea[:, c * CHUNK : (c + 1) * CHUNK])
            if c == 0:
                nc.sync.dma_start(w1_sb[:], w1)
        b1_sb = held.tile([P, 1], F32, name="b1_sb")
        nc.sync.dma_start(b1_sb[:], b1)
        wenv_sb = held.tile([P, P], BF16, name="wenv_sb")
        nc.sync.dma_start(wenv_sb[:], wenv)
        rbf_sb = held.tile([P, PIECES, BANK], BF16, name="rbf_sb")
        rbf_pieces = rbf.rearrange("q (n h a) -> q h n a", n=NEIGHBOURS, h=HALVES)
        offsets = held.tile([P, ENTRIES // ENTRIES_PER_OFFSET_COLUMN], U16, name="offsets")
        nc.sync.dma_start(rbf_sb[:, 0, :], rbf_pieces[:, 0, 0, :])
        nc.sync.dma_start(offsets[:], offs)
        nc.sync.dma_start(rbf_sb[:, 1, :], rbf_pieces[:, 0, 1, :])
        for k in range(2, PIECES, 2):
            h, n = divmod(k, NEIGHBOURS)
            nc.sync.dma_start(rbf_sb[:, k : k + 2, :], rbf_pieces[:, h, n : n + 2, :])

        identity = held.tile([P, P], F32, name="identity")
        make_identity(nc, identity[:])

        warm_ps = banks.tile([P, P], F32, name="warm_ps", tag="bank")
        for repeat in range(WARM_UP_MATMULS):
            nc.tensor.matmul(warm_ps[:], identity[:], identity[:], start=True, stop=True)

        t = held.tile([P, ATOMS], F32, name="t")
        for c in range(CHUNKS):
            act = per_chunk.tile([P, CHUNK], BF16, name="act")
            nc.scalar.activation(act[:], fea[c][:], SILU)
            for first, width in spans([CHUNK]) if c < CHUNKS - 1 else spans(LAST_CHUNK_PARTS):
                t_ps = banks.tile([P, CHUNK], F32, name="t_ps", tag="bank")
                nc.tensor.matmul(t_ps[:, :width], w1_sb[:], act[:, first : first + width], start=True, stop=True)
                t_part = t[:, c * CHUNK + first : c * CHUNK + first + width]
                if first == 0:
                    nc.vector.tensor_scalar(t_part, t_ps[:, :width], b1_sb[:, 0:1], None, ADD)
                else:
                    nc.scalar.activation(t_part, t_ps[:, :width], IDENTITY, bias=b1_sb[:, 0:1])

        env = []
        for k in range(PIECES):
            env.append(per_piece.tile([P, BANK], F32, name="env"))
            for first, width in parts_of(k):
                env_ps = banks.tile([P, BANK], F32, name="env_ps", tag="bank")
                nc.tensor.matmul(env_ps[:, :width], wenv_sb[:], rbf_sb[:, k, first : first + width], start=True, stop=True)
                nc.scalar.copy(env[k][:, first : first + width], env_ps[:, :width])

        for k in range(PIECES):
            h, n = divmod(k, NEIGHBOURS)
            if n == 0:
                sums = [banks.tile([P, BANK], F32, name="sums", tag="bank") for group in groups_of(h)]
                out_sb = per_half.tile([P, BANK], F32, name="out_sb")
            prod = per_piece.tile([P, BANK], F32, name="prod")
            for first, width in parts_of(k):
                column = (n * ATOMS + h * BANK + first) // ENTRIES_PER_OFFSET_COLUMN
                picked = t[:].indirect(offsets[:, column : column + width // ENTRIES_PER_OFFSET_COLUMN])
                nc.vector.tensor_tensor(prod[:, first : first + width], picked, env[k][:, first : first + width], MULT)
            for g, (first, width) in enumerate(groups_of(h)):
                group_sum = sums[g][:, :width]
                group_prod = prod[:, first : first + width]
                group_out = out_sb[:, first : first + width]
                if k < PIECES - 1:
                    closes = n == NEIGHBOURS - 1 or k == PIECES - 2
                    nc.tensor.matmul(group_sum, identity[:], group_prod, start=(n == 0), stop=closes)
                if n == NEIGHBOURS - 1:
                    if k < PIECES - 1:
                        nc.scalar.copy(group_out, group_sum)
                    else:
                        nc.vector.tensor_tensor(group_out, group_sum, group_prod, ADD)
                    atom = h * BANK + first
                    nc.sync.dma_start(out[:, atom : atom + width], group_out)
